import numpy as np
import ml_dtypes


def mxq(x, axis, fmt="e4m3"):
    dtype, down = {"e4m3": (ml_dtypes.float8_e4m3fn, 7), "e5m2": (ml_dtypes.float8_e5m2, 14)}[fmt]
    v = np.moveaxis(np.asarray(x, np.float32).astype(ml_dtypes.bfloat16).astype(np.float64), axis, -1)
    blocks = v.reshape(v.shape[:-1] + (-1, 32))
    amax = np.abs(blocks).max(-1, keepdims=True)
    byte = np.maximum(np.where(amax > 0, np.frexp(amax)[1] - 1 + 127, 0) - down, 1)
    scale = np.exp2(byte - 127.0)
    codes = (blocks / scale).astype(np.float32).astype(dtype).astype(np.float64)
    return np.moveaxis((codes * scale).reshape(v.shape), -1, axis)


WIDE = False


def mx_kscale(k):
    if not WIDE:
        return np.ones(k)
    levels = np.array([10, -10, 5, -5, 0])
    if k % 512:
        return np.exp2(np.random.permutation(np.resize(levels, k // 32))).repeat(32)
    a = np.empty((k // 512, 16))
    for p in range(k // 512):
        a[p, :8] = np.random.permutation(np.resize(levels, 8))
        for g in range(8):
            far = levels[np.abs(levels - a[p, g]) >= 10]
            a[p, g + 8] = far[np.random.randint(len(far))]
    return np.exp2(a.ravel()).repeat(32)


BF16 = ml_dtypes.bfloat16


def bf(x):
    return np.asarray(x, np.float32).astype(BF16)


def f64(x):
    return np.asarray(x).astype(np.float64)


B, S, D_IN, D_OUT, R = 4, 256, 1024, 1024, 128
SCALING = 2.0


def setup_inputs():
    s = mx_kscale(D_IN)
    g = np.sqrt(np.mean(1.0 / (s * s)))
    return {"x": bf(np.random.standard_normal((B, S, D_IN)) * s),
            "weight": bf(np.random.standard_normal((D_OUT, D_IN)) / np.sqrt(D_IN) / s),
            "a_w": bf(np.random.standard_normal((R, D_IN)) / np.sqrt(D_IN) / s),
            "b_w": bf(np.random.standard_normal((D_OUT, R)) / np.sqrt(R)),
            "magnitude": bf((np.random.uniform(size=(1, D_OUT)) + 0.5) * g),
            "h_lora": bf(np.random.standard_normal((B, S, R)))}


def reference(x, weight, a_w, b_w, magnitude, h_lora):
    w = f64(weight)
    base_out = mxq(f64(x), 2, "e4m3") @ mxq(w, 1, "e4m3").T
    lora_out = SCALING * (f64(h_lora) @ f64(b_w).T)
    w_eff = w + SCALING * (f64(b_w) @ f64(a_w))
    weight_norm = np.sqrt((w_eff * w_eff).sum(axis=1))
    mag_norm_scale = (f64(magnitude) / weight_norm).reshape(1, 1, -1)
    dora_out = (mag_norm_scale - 1.0) * base_out + mag_norm_scale * lora_out
    return base_out + dora_out

@@ -1,0 +1,294 @@
+from contextlib import ExitStack
+
+import concourse.mybir as mybir
+from concourse.masks import make_identity
+
+F32 = mybir.dt.float32
+BF16 = mybir.dt.bfloat16
+U32 = mybir.dt.uint32
+U8 = mybir.dt.uint8
+FP8X4 = mybir.dt.float8_e4m3fn_x4
+ACT = mybir.ActivationFunctionType
+ALU = mybir.AluOpType
+
+P = 128
+PACK = 4
+BANK = 512
+
+TOKENS = 1024
+D_IN = 1024
+D_OUT = 1024
+RANK = 128
+SCALING = 2.0
+
+T_TILES = TOKENS // P
+O_TILES = D_OUT // P
+PASSES = D_IN // (P * PACK)
+HALVES = D_OUT // BANK
+O_TILES_PER_HALF = BANK // P
+WORD_BLOCKS = D_IN // 2 // P
+
+EARLY = 2
+SCALE_LAG = 1
+SCALAR_W_BANKS = 2
+TILES_MERGED_ON_TENSOR = 3
+
+FLOPS = 2 * TOKENS * D_IN * D_OUT + 2 * TOKENS * RANK * D_OUT + 2 * D_OUT * RANK * D_IN
+
+
+def merged_on_tensor(j):
+    return O_TILES - 1 - TILES_MERGED_ON_TENSOR <= j < O_TILES - 1
+
+
+def tile_loralinear_pa_kernel(tc, x, weight, a_w, b_w, magnitude, h_lora, out):
+    nc = tc.nc
+    x_rows = x.flatten_outer_dims().rearrange("(p i) d -> p i d", i=T_TILES)
+    h_rows = h_lora.flatten_outer_dims().rearrange("(p i) r -> p i r", i=T_TILES)
+    out_rows = out.flatten_outer_dims().rearrange("(p i) o -> p i o", i=T_TILES)
+
+    with ExitStack() as ctx:
+        keep = ctx.enter_context(tc.tile_pool(name="keep", bufs=1))
+        merged = ctx.enter_context(tc.tile_pool(name="merged", bufs=4))
+        psum = ctx.enter_context(tc.psum_pool(name="psum", bufs=7))
+        psum_kept = ctx.enter_context(tc.psum_pool(name="psum_kept", bufs=1))
+        ctx.enter_context(tc.manual_schedule())
+
+        ident_bf16 = keep.tile([P, P], BF16)
+        make_identity(nc, ident_bf16[:])
+        ident_f32 = keep.tile([P, P], F32)
+        make_identity(nc, ident_f32[:])
+        table_warmer = keep.tile([P, 1], F32)
+        nc.vector.memset(table_warmer[:], 1.0)
+        nc.scalar.sqrt(table_warmer[:], table_warmer[:])
+        mag_rows = keep.tile([P, P], BF16)
+        nc.vector.memset(mag_rows[:], 0.0)
+
+        b_sb = keep.tile([P, O_TILES, RANK], BF16)
+        nc.sync.dma_start(out=b_sb[:], in_=b_w.rearrange("(j p) r -> p j r", p=P))
+        a_sb = keep.tile([P, D_IN], BF16)
+        nc.sync.dma_start(out=a_sb[:], in_=a_w)
+        w_sb = keep.tile([P, O_TILES, D_IN], BF16)
+        for j in range(O_TILES):
+            nc.sync.dma_start(out=w_sb[:, j, :], in_=weight[j * P : (j + 1) * P, :])
+        h_sb = keep.tile([P, T_TILES, RANK], BF16)
+        nc.sync.dma_start(out=h_sb[:], in_=h_rows)
+        x_sb = keep.tile([P, T_TILES, D_IN], BF16)
+        for i in range(0, T_TILES, 2):
+            nc.sync.dma_start(out=x_sb[:, i : i + 2, :], in_=x_rows[:, i : i + 2, :])
+        nc.sync.dma_start(
+            out=mag_rows[0:O_TILES, :], in_=magnitude.rearrange("one (j p) -> (one j) p", p=P)
+        )
+        w_words = w_sb[:].bitcast(F32)
+        x_words = x_sb[:].bitcast(F32)
+
+        b2T = keep.tile([P, D_OUT], BF16)
+        hT = keep.tile([P, T_TILES, P], BF16)
+        w_grouped = keep.tile([P, HALVES, PASSES, BANK, PACK], BF16, align_bytes=64)
+        w_grouped_words = w_grouped[:].bitcast(F32)
+        w_codes = keep.tile([P, HALVES, PASSES, BANK], U32, align_bytes=64)
+        w_scales = keep.tile([P, HALVES, PASSES, BANK], U8, align_bytes=64)
+        x_grouped = keep.tile([P, T_TILES, PASSES, P, PACK], BF16, align_bytes=64)
+        x_grouped_words = x_grouped[:].bitcast(F32)
+        x_codes = keep.tile([P, T_TILES, PASSES, P], U32, align_bytes=64)
+        x_scales = keep.tile([P, T_TILES, PASSES, P], U8, align_bytes=64)
+        norm_sq_parts = keep.tile([P, D_IN // BANK, O_TILES], F32)
+        nc.vector.memset(norm_sq_parts[:], 0.0)
+        m_first = keep.tile([P, BANK], F32)
+        m_second = psum_kept.tile([P, O_TILES_PER_HALF, P], F32)
+        results = keep.tile([P, T_TILES, D_OUT], F32)
+
+        def turn_words(row_words):
+            bank = psum.tile([P, WORD_BLOCKS, P], F32, tag="bank")
+            for blk in range(WORD_BLOCKS):
+                g, u = divmod(blk, 2)
+                nc.tensor.transpose(
+                    bank[:, blk, :],
+                    row_words[:, 2 * P * g + u : 2 * P * (g + 1) : 2],
+                    ident_f32[:],
+                )
+            return bank
+
+        def group_words(on_vector, grouped_words, bank):
+            side_by_side = bank[:].rearrange("p (g u) r -> p g r u", u=2)
+            if on_vector:
+                nc.vector.tensor_copy(out=grouped_words, in_=side_by_side)
+            else:
+                nc.scalar.copy(out=grouped_words, in_=side_by_side)
+
+        def group_weight_words(j, bank):
+            half, j_in_half = divmod(j, O_TILES_PER_HALF)
+            group_words(
+                j >= SCALAR_W_BANKS,
+                w_grouped_words[:, half, :, j_in_half * P : (j_in_half + 1) * P, :],
+                bank,
+            )
+
+        def quantise_weight(half):
+            nc.vector.quantize_mx(
+                out=w_codes[:, half, :, :].rearrange("p g o -> p (g o)").bitcast(FP8X4),
+                scales=w_scales[:, half, :, :].rearrange("p g o -> p (g o)"),
+                in_=w_grouped[:, half, :, :, :].rearrange("p g o t -> p (g o t)"),
+            )
+
+        def quantise_tokens(i):
+            nc.vector.quantize_mx(
+                out=x_codes[:, i, :, :].rearrange("p g r -> p (g r)").bitcast(FP8X4),
+                scales=x_scales[:, i, :, :].rearrange("p g r -> p (g r)"),
+                in_=x_grouped[:, i, :, :, :].rearrange("p g r t -> p (g r t)"),
+            )
+
+        def adapter_weight_products(j):
+            banks = []
+            for c in range(D_IN // BANK):
+                cols = slice(c * BANK, (c + 1) * BANK)
+                ba2 = psum.tile([P, BANK], F32, tag="bank", name="ba2")
+                if merged_on_tensor(j):
+                    nc.tensor.matmul(
+                        out=ba2[:], lhsT=ident_bf16[:], rhs=w_sb[:, j, cols], start=True, stop=False
+                    )
+                nc.tensor.matmul(
+                    out=ba2[:], lhsT=b2T[:, j * P : (j + 1) * P], rhs=a_sb[:, cols],
+                    start=(not merged_on_tensor(j)), stop=True,
+                )
+                banks.append(ba2)
+            return banks
+
+        def merge_weight(j, banks, w_eff):
+            for c in range(D_IN // BANK):
+                cols = slice(c * BANK, (c + 1) * BANK)
+                nc.vector.tensor_tensor(
+                    out=w_eff[:, cols], in0=banks[c][:], in1=w_sb[:, j, cols], op=ALU.add
+                )
+
+        def sum_squares(j, banks, w_eff):
+            if merged_on_tensor(j):
+                for c in range(D_IN // BANK):
+                    nc.scalar.activation(
+                        out=w_eff[:, c * BANK : (c + 1) * BANK], in_=banks[c][:], func=ACT.Square,
+                        accum_out=norm_sq_parts[:, c, j : j + 1],
+                    )
+            else:
+                nc.scalar.activation(
+                    out=w_eff[:], in_=w_eff[:], func=ACT.Square,
+                    accum_out=norm_sq_parts[:, 0, j : j + 1],
+                )
+
+        def lora_products(i):
+            for half in range(HALVES):
+                cols = slice(half * BANK, (half + 1) * BANK)
+                lora = psum.tile([P, BANK], F32, tag="bank")
+                nc.tensor.matmul(
+                    out=lora[:], lhsT=hT[:, i, :], rhs=b2T[:, cols], start=True, stop=True
+                )
+                nc.scalar.copy(out=results[:, i, cols], in_=lora[:])
+
+        def add_base_products(i):
+            for half in range(HALVES):
+                cols = slice(half * BANK, (half + 1) * BANK)
+                base = psum.tile([P, BANK], F32, tag="bank")
+                for g in range(PASSES):
+                    nc.tensor.matmul_mx(
+                        out=base[:],
+                        lhsT=x_codes[:, i, g, :].bitcast(FP8X4),
+                        lhsT_scale=x_scales[:, i, g, :],
+                        rhs=w_codes[:, half, g, :].bitcast(FP8X4),
+                        rhs_scale=w_scales[:, half, g, :],
+                        start=(g == 0),
+                        stop=(g == PASSES - 1),
+                    )
+                nc.vector.tensor_tensor(
+                    out=results[:, i, cols], in0=base[:], in1=results[:, i, cols], op=ALU.add
+                )
+
+        def scale_and_store(i):
+            nc.gpsimd.tensor_tensor(
+                out=results[:, i, 0:BANK], in0=results[:, i, 0:BANK], in1=m_first[:], op=ALU.mult
+            )
+            nc.sync.dma_start(out=out_rows[:, i, 0:BANK], in_=results[:, i, 0:BANK])
+            nc.vector.tensor_tensor(
+                out=results[:, i, BANK:D_OUT],
+                in0=m_second[:].rearrange("p j o -> p (j o)"),
+                in1=results[:, i, BANK:D_OUT],
+                op=ALU.mult,
+            )
+            nc.sync.dma_start(out=out_rows[:, i, BANK:D_OUT], in_=results[:, i, BANK:D_OUT])
+
+        for half in range(HALVES):
+            b_turned = psum.tile([P, O_TILES_PER_HALF, P], BF16, tag="bank")
+            for j_in_half in range(O_TILES_PER_HALF):
+                nc.tensor.transpose(
+                    b_turned[:, j_in_half, :],
+                    b_sb[:, half * O_TILES_PER_HALF + j_in_half, :],
+                    ident_bf16[:],
+                )
+            nc.scalar.mul(
+                out=b2T[:, half * BANK : (half + 1) * BANK],
+                in_=b_turned[:].rearrange("r j o -> r (j o)"),
+                mul=SCALING,
+            )
+
+        for j in range(O_TILES):
+            ba2_banks = adapter_weight_products(j)
+            w_turned = turn_words(w_words[:, j, :])
+            w_eff = merged.tile([P, D_IN], F32)
+            if not merged_on_tensor(j):
+                merge_weight(j, ba2_banks, w_eff)
+            group_weight_words(j, w_turned)
+            if j == O_TILES - 1 - EARLY:
+                h_turned = psum.tile([P, T_TILES, P], BF16, tag="bank")
+                for i in range(T_TILES):
+                    nc.tensor.transpose(h_turned[:, i, :], h_sb[:, i, :], ident_bf16[:])
+                nc.scalar.copy(out=hT[:], in_=h_turned[:])
+            if j >= O_TILES - EARLY:
+                i = j - (O_TILES - EARLY)
+                group_words(False, x_grouped_words[:, i, :, :, :], turn_words(x_words[:, i, :]))
+            sum_squares(j, ba2_banks, w_eff)
+            if j == O_TILES_PER_HALF:
+                quantise_weight(0)
+
+        mag_turned = psum.tile([P, P], BF16, tag="bank")
+        nc.tensor.transpose(mag_turned[:], mag_rows[:], ident_bf16[:])
+        mag_col = keep.tile([P, O_TILES], F32)
+        nc.vector.tensor_copy(out=mag_col[:], in_=mag_turned[:, 0:O_TILES])
+
+        quantise_tokens(0)
+        quantise_weight(1)
+        for i in range(1, EARLY):
+            quantise_tokens(i)
+        norm_sq = keep.tile([P, O_TILES], F32)
+        nc.vector.tensor_tensor(
+            out=norm_sq[:], in0=norm_sq_parts[:, 0, :], in1=norm_sq_parts[:, 1, :], op=ALU.add
+        )
+        norm = keep.tile([P, O_TILES], F32)
+
+        for i in range(T_TILES + SCALE_LAG):
+            if i < T_TILES:
+                lora_products(i)
+                if i == 0:
+                    nc.scalar.sqrt(norm[:], norm_sq[:])
+                if i + EARLY < T_TILES:
+                    group_words(
+                        False,
+                        x_grouped_words[:, i + EARLY, :, :, :],
+                        turn_words(x_words[:, i + EARLY, :]),
+                    )
+                add_base_products(i)
+                if i + EARLY < T_TILES:
+                    quantise_tokens(i + EARLY)
+            if i == 0:
+                inv_norm = keep.tile([P, O_TILES], F32)
+                nc.vector.reciprocal(out=inv_norm[:], in_=norm[:])
+                m_col = keep.tile([P, O_TILES], F32)
+                nc.vector.tensor_tensor(out=m_col[:], in0=inv_norm[:], in1=mag_col[:], op=ALU.mult)
+            if i == 1:
+                m_turned = psum.tile([P, O_TILES_PER_HALF, P], F32, tag="bank")
+                for j in range(O_TILES):
+                    half, j_in_half = divmod(j, O_TILES_PER_HALF)
+                    nc.tensor.transpose(
+                        (m_turned, m_second)[half][:, j_in_half, :],
+                        m_col[:, j : j + 1].to_broadcast([P, P]),
+                        ident_f32[:],
+                    )
+                nc.scalar.copy(out=m_first[:], in_=m_turned[:].rearrange("p j o -> p (j o)"))
+            if i >= SCALE_LAG:
+                scale_and_store(i - SCALE_LAG)

@@ -28,23 +28,24 @@ HALVES = D_OUT // BANK
 O_TILES_PER_HALF = BANK // P
 WORD_BLOCKS = D_IN // 2 // P
 
-EARLY = 2
-SCALE_LAG = 1
-SCALAR_W_BANKS = 2
-TILES_MERGED_ON_TENSOR = 3
+STRIDED_W = 2
+STRIDED_X = 0
+MERGED = (4, 5, 6, 7)
+SCALAR_W = (0, 1)
+VECTOR_X = (0,)
+G_COLS = 640
+EARLY = 4
+LATE = 0
+W_BEFORE_X = 8
 
 FLOPS = 2 * TOKENS * D_IN * D_OUT + 2 * TOKENS * RANK * D_OUT + 2 * D_OUT * RANK * D_IN
-
-
-def merged_on_tensor(j):
-    return O_TILES - 1 - TILES_MERGED_ON_TENSOR <= j < O_TILES - 1
-
 
 def tile_loralinear_pa_kernel(tc, x, weight, a_w, b_w, magnitude, h_lora, out):
     nc = tc.nc
     x_rows = x.flatten_outer_dims().rearrange("(p i) d -> p i d", i=T_TILES)
     h_rows = h_lora.flatten_outer_dims().rearrange("(p i) r -> p i r", i=T_TILES)
     out_rows = out.flatten_outer_dims().rearrange("(p i) o -> p i o", i=T_TILES)
+    b_rows = b_w.rearrange("(j p) r -> p j r", p=P)
 
     with ExitStack() as ctx:
         keep = ctx.enter_context(tc.tile_pool(name="keep", bufs=1))
@@ -64,25 +65,41 @@ def tile_loralinear_pa_kernel(tc, x, weight, a_w, b_w, magnitude, h_lora, out):
         nc.vector.memset(mag_rows[:], 0.0)
 
         b_sb = keep.tile([P, O_TILES, RANK], BF16)
-        nc.sync.dma_start(out=b_sb[:], in_=b_w.rearrange("(j p) r -> p j r", p=P))
         a_sb = keep.tile([P, D_IN], BF16)
-        nc.sync.dma_start(out=a_sb[:], in_=a_w)
         w_sb = keep.tile([P, O_TILES, D_IN], BF16)
-        for j in range(O_TILES):
-            nc.sync.dma_start(out=w_sb[:, j, :], in_=weight[j * P : (j + 1) * P, :])
         h_sb = keep.tile([P, T_TILES, RANK], BF16)
-        nc.sync.dma_start(out=h_sb[:], in_=h_rows)
         x_sb = keep.tile([P, T_TILES, D_IN], BF16)
-        for i in range(0, T_TILES, 2):
-            nc.sync.dma_start(out=x_sb[:, i : i + 2, :], in_=x_rows[:, i : i + 2, :])
+
+        def load_w(j):
+            nc.sync.dma_start(out=w_sb[:, j, :], in_=weight[j * P : (j + 1) * P, :])
+
+        def load_x(i, n):
+            nc.sync.dma_start(out=x_sb[:, i : i + n, :], in_=x_rows[:, i : i + n, :])
+
+        nc.sync.dma_start(out=b_sb[:, 0:4, :], in_=b_rows[:, 0:4, :])
+        load_w(0)
+        nc.sync.dma_start(out=a_sb[:], in_=a_w)
+        load_w(1)
+        nc.sync.dma_start(out=b_sb[:, 4:8, :], in_=b_rows[:, 4:8, :])
+        for j in range(2, W_BEFORE_X):
+            load_w(j)
+        nc.sync.dma_start(out=h_sb[:], in_=h_rows)
+        load_x(0, 1)
+        load_x(1, 1)
+        for j in range(W_BEFORE_X, O_TILES):
+            load_w(j)
         nc.sync.dma_start(
             out=mag_rows[0:O_TILES, :], in_=magnitude.rearrange("one (j p) -> (one j) p", p=P)
         )
-        w_words = w_sb[:].bitcast(F32)
-        x_words = x_sb[:].bitcast(F32)
+        for i in (2, 4, 6):
+            load_x(i, 2)
+        w_words = w_sb[:].bitcast(U32)
+        x_words = x_sb[:].bitcast(U32)
 
         b2T = keep.tile([P, D_OUT], BF16)
         hT = keep.tile([P, T_TILES, P], BF16)
+        w_ordered = keep.tile([P, O_TILES, D_IN // 2], U32)
+        x_ordered = keep.tile([P, T_TILES, D_IN // 2], U32)
         w_grouped = keep.tile([P, HALVES, PASSES, BANK, PACK], BF16, align_bytes=64)
         w_grouped_words = w_grouped[:].bitcast(F32)
         w_codes = keep.tile([P, HALVES, PASSES, BANK], U32, align_bytes=64)
@@ -93,18 +110,32 @@ def tile_loralinear_pa_kernel(tc, x, weight, a_w, b_w, magnitude, h_lora, out):
         x_scales = keep.tile([P, T_TILES, PASSES, P], U8, align_bytes=64)
         norm_sq_parts = keep.tile([P, D_IN // BANK, O_TILES], F32)
         nc.vector.memset(norm_sq_parts[:], 0.0)
-        m_first = keep.tile([P, BANK], F32)
+        m_sb = keep.tile([P, G_COLS], F32)
         m_second = psum_kept.tile([P, O_TILES_PER_HALF, P], F32)
         results = keep.tile([P, T_TILES, D_OUT], F32)
 
-        def turn_words(row_words):
+        def order_words(ordered, words):
+            nc.gpsimd.tensor_copy(
+                out=ordered.rearrange("p (g u q) -> p g u q", g=PASSES, u=2),
+                in_=words.rearrange("p (g q u) -> p g u q", g=PASSES, u=2),
+            )
+
+        def turn_ordered(ordered):
             bank = psum.tile([P, WORD_BLOCKS, P], F32, tag="bank")
+            ordered = ordered.bitcast(F32)
+            for blk in range(WORD_BLOCKS):
+                nc.tensor.transpose(
+                    bank[:, blk, :], ordered[:, blk * P : (blk + 1) * P], ident_f32[:]
+                )
+            return bank
+
+        def turn_strided(words):
+            bank = psum.tile([P, WORD_BLOCKS, P], F32, tag="bank")
+            words = words.bitcast(F32)
             for blk in range(WORD_BLOCKS):
                 g, u = divmod(blk, 2)
                 nc.tensor.transpose(
-                    bank[:, blk, :],
-                    row_words[:, 2 * P * g + u : 2 * P * (g + 1) : 2],
-                    ident_f32[:],
+                    bank[:, blk, :], words[:, 2 * P * g + u : 2 * P * (g + 1) : 2], ident_f32[:]
                 )
             return bank
 
@@ -115,13 +146,18 @@ def tile_loralinear_pa_kernel(tc, x, weight, a_w, b_w, magnitude, h_lora, out):
             else:
                 nc.scalar.copy(out=grouped_words, in_=side_by_side)
 
-        def group_weight_words(j, bank):
-            half, j_in_half = divmod(j, O_TILES_PER_HALF)
-            group_words(
-                j >= SCALAR_W_BANKS,
-                w_grouped_words[:, half, :, j_in_half * P : (j_in_half + 1) * P, :],
-                bank,
-            )
+        def turn_w(j):
+            return turn_strided(w_words[:, j, :]) if j < STRIDED_W else turn_ordered(w_ordered[:, j, :])
+
+        def turn_x(i):
+            return turn_strided(x_words[:, i, :]) if i < STRIDED_X else turn_ordered(x_ordered[:, i, :])
+
+        def group_w(j, bank):
+            half, jh = divmod(j, O_TILES_PER_HALF)
+            group_words(j not in SCALAR_W, w_grouped_words[:, half, :, jh * P : (jh + 1) * P, :], bank)
+
+        def group_x(i, bank):
+            group_words(i in VECTOR_X, x_grouped_words[:, i, :, :, :], bank)
 
         def quantise_weight(half):
             nc.vector.quantize_mx(
@@ -137,18 +173,18 @@ def tile_loralinear_pa_kernel(tc, x, weight, a_w, b_w, magnitude, h_lora, out):
                 in_=x_grouped[:, i, :, :, :].rearrange("p g r t -> p (g r t)"),
             )
 
-        def adapter_weight_products(j):
+        def products(j):
             banks = []
             for c in range(D_IN // BANK):
                 cols = slice(c * BANK, (c + 1) * BANK)
                 ba2 = psum.tile([P, BANK], F32, tag="bank", name="ba2")
-                if merged_on_tensor(j):
+                if j in MERGED:
                     nc.tensor.matmul(
                         out=ba2[:], lhsT=ident_bf16[:], rhs=w_sb[:, j, cols], start=True, stop=False
                     )
                 nc.tensor.matmul(
                     out=ba2[:], lhsT=b2T[:, j * P : (j + 1) * P], rhs=a_sb[:, cols],
-                    start=(not merged_on_tensor(j)), stop=True,
+                    start=(j not in MERGED), stop=True,
                 )
                 banks.append(ba2)
             return banks
@@ -161,7 +197,7 @@ def tile_loralinear_pa_kernel(tc, x, weight, a_w, b_w, magnitude, h_lora, out):
                 )
 
         def sum_squares(j, banks, w_eff):
-            if merged_on_tensor(j):
+            if j in MERGED:
                 for c in range(D_IN // BANK):
                     nc.scalar.activation(
                         out=w_eff[:, c * BANK : (c + 1) * BANK], in_=banks[c][:], func=ACT.Square,
@@ -173,122 +209,144 @@ def tile_loralinear_pa_kernel(tc, x, weight, a_w, b_w, magnitude, h_lora, out):
                     accum_out=norm_sq_parts[:, 0, j : j + 1],
                 )
 
-        def lora_products(i):
-            for half in range(HALVES):
-                cols = slice(half * BANK, (half + 1) * BANK)
-                lora = psum.tile([P, BANK], F32, tag="bank")
-                nc.tensor.matmul(
-                    out=lora[:], lhsT=hT[:, i, :], rhs=b2T[:, cols], start=True, stop=True
-                )
-                nc.scalar.copy(out=results[:, i, cols], in_=lora[:])
+        def lora(i, half):
+            cols = slice(half * BANK, (half + 1) * BANK)
+            bank = psum.tile([P, BANK], F32, tag="bank")
+            nc.tensor.matmul(out=bank[:], lhsT=hT[:, i, :], rhs=b2T[:, cols], start=True, stop=True)
+            return bank
 
-        def add_base_products(i):
-            for half in range(HALVES):
-                cols = slice(half * BANK, (half + 1) * BANK)
-                base = psum.tile([P, BANK], F32, tag="bank")
-                for g in range(PASSES):
-                    nc.tensor.matmul_mx(
-                        out=base[:],
-                        lhsT=x_codes[:, i, g, :].bitcast(FP8X4),
-                        lhsT_scale=x_scales[:, i, g, :],
-                        rhs=w_codes[:, half, g, :].bitcast(FP8X4),
-                        rhs_scale=w_scales[:, half, g, :],
-                        start=(g == 0),
-                        stop=(g == PASSES - 1),
-                    )
-                nc.vector.tensor_tensor(
-                    out=results[:, i, cols], in0=base[:], in1=results[:, i, cols], op=ALU.add
+        def lora_out(i, half, bank):
+            nc.scalar.copy(out=results[:, i, half * BANK : (half + 1) * BANK], in_=bank[:])
+
+        def base(i, half):
+            bank = psum.tile([P, BANK], F32, tag="bank")
+            for g in range(PASSES):
+                nc.tensor.matmul_mx(
+                    out=bank[:],
+                    lhsT=x_codes[:, i, g, :].bitcast(FP8X4),
+                    lhsT_scale=x_scales[:, i, g, :],
+                    rhs=w_codes[:, half, g, :].bitcast(FP8X4),
+                    rhs_scale=w_scales[:, half, g, :],
+                    start=(g == 0),
+                    stop=(g == PASSES - 1),
                 )
+            return bank
+
+        def add_base(i, half, bank):
+            cols = slice(half * BANK, (half + 1) * BANK)
+            nc.vector.tensor_tensor(
+                out=results[:, i, cols], in0=bank[:], in1=results[:, i, cols], op=ALU.add
+            )
 
         def scale_and_store(i):
+            split = G_COLS if i < T_TILES - 1 else BANK
             nc.gpsimd.tensor_tensor(
-                out=results[:, i, 0:BANK], in0=results[:, i, 0:BANK], in1=m_first[:], op=ALU.mult
+                out=results[:, i, 0:split], in0=results[:, i, 0:split], in1=m_sb[:, 0:split], op=ALU.mult
             )
-            nc.sync.dma_start(out=out_rows[:, i, 0:BANK], in_=results[:, i, 0:BANK])
+            nc.sync.dma_start(out=out_rows[:, i, 0:split], in_=results[:, i, 0:split])
             nc.vector.tensor_tensor(
-                out=results[:, i, BANK:D_OUT],
-                in0=m_second[:].rearrange("p j o -> p (j o)"),
-                in1=results[:, i, BANK:D_OUT],
+                out=results[:, i, split:D_OUT],
+                in0=m_second[:].rearrange("p j o -> p (j o)")[:, split - BANK : BANK],
+                in1=results[:, i, split:D_OUT],
                 op=ALU.mult,
             )
-            nc.sync.dma_start(out=out_rows[:, i, BANK:D_OUT], in_=results[:, i, BANK:D_OUT])
+            nc.sync.dma_start(out=out_rows[:, i, split:D_OUT], in_=results[:, i, split:D_OUT])
 
-        for half in range(HALVES):
+        def turn_b(half):
             b_turned = psum.tile([P, O_TILES_PER_HALF, P], BF16, tag="bank")
-            for j_in_half in range(O_TILES_PER_HALF):
+            for jh in range(O_TILES_PER_HALF):
                 nc.tensor.transpose(
-                    b_turned[:, j_in_half, :],
-                    b_sb[:, half * O_TILES_PER_HALF + j_in_half, :],
-                    ident_bf16[:],
+                    b_turned[:, jh, :], b_sb[:, half * O_TILES_PER_HALF + jh, :], ident_bf16[:]
                 )
-            nc.scalar.mul(
+            nc.vector.tensor_scalar(
                 out=b2T[:, half * BANK : (half + 1) * BANK],
-                in_=b_turned[:].rearrange("r j o -> r (j o)"),
-                mul=SCALING,
+                in0=b_turned[:].rearrange("r j o -> r (j o)"),
+                scalar1=SCALING, scalar2=None, op0=ALU.mult,
             )
 
-        for j in range(O_TILES):
-            ba2_banks = adapter_weight_products(j)
-            w_turned = turn_words(w_words[:, j, :])
+        norm_sq = keep.tile([P, O_TILES], F32)
+        norm = keep.tile([P, O_TILES], F32)
+        inv_norm = keep.tile([P, O_TILES], F32)
+        m_col = keep.tile([P, O_TILES], F32)
+        mag_col = keep.tile([P, O_TILES], F32)
+
+        for j in range(STRIDED_W, O_TILES):
+            order_words(w_ordered[:, j, :], w_words[:, j, :])
+        for i in range(STRIDED_X, T_TILES):
+            order_words(x_ordered[:, i, :], x_words[:, i, :])
+
+        late = []
+
+        def flush(n=0):
+            while len(late) > n:
+                sum_squares(*late.pop(0))
+
+        def weight_step(j):
+            w_turned = turn_w(j)
+            if j == 1:
+                turn_b(1)
+            banks = products(j)
             w_eff = merged.tile([P, D_IN], F32)
-            if not merged_on_tensor(j):
-                merge_weight(j, ba2_banks, w_eff)
-            group_weight_words(j, w_turned)
-            if j == O_TILES - 1 - EARLY:
+            group_w(j, w_turned)
+            if j not in MERGED:
+                merge_weight(j, banks, w_eff)
+                late.append((j, banks, w_eff))
+                flush(LATE)
+            else:
+                flush(LATE)
+                sum_squares(j, banks, w_eff)
+
+        turn_b(0)
+        for j in range(O_TILES):
+            weight_step(j)
+            if j == 4:
+                quantise_weight(0)
+            if j == 5:
                 h_turned = psum.tile([P, T_TILES, P], BF16, tag="bank")
                 for i in range(T_TILES):
                     nc.tensor.transpose(h_turned[:, i, :], h_sb[:, i, :], ident_bf16[:])
-                nc.scalar.copy(out=hT[:], in_=h_turned[:])
-            if j >= O_TILES - EARLY:
-                i = j - (O_TILES - EARLY)
-                group_words(False, x_grouped_words[:, i, :, :, :], turn_words(x_words[:, i, :]))
-            sum_squares(j, ba2_banks, w_eff)
-            if j == O_TILES_PER_HALF:
-                quantise_weight(0)
-
+                nc.vector.tensor_copy(out=hT[:], in_=h_turned[:])
+        for i in range(EARLY):
+            group_x(i, turn_x(i))
+        flush(0)
         mag_turned = psum.tile([P, P], BF16, tag="bank")
         nc.tensor.transpose(mag_turned[:], mag_rows[:], ident_bf16[:])
-        mag_col = keep.tile([P, O_TILES], F32)
-        nc.vector.tensor_copy(out=mag_col[:], in_=mag_turned[:, 0:O_TILES])
-
+        lora_out(0, 0, lora(0, 0))
         quantise_tokens(0)
         quantise_weight(1)
-        for i in range(1, EARLY):
-            quantise_tokens(i)
-        norm_sq = keep.tile([P, O_TILES], F32)
         nc.vector.tensor_tensor(
             out=norm_sq[:], in0=norm_sq_parts[:, 0, :], in1=norm_sq_parts[:, 1, :], op=ALU.add
         )
-        norm = keep.tile([P, O_TILES], F32)
-
-        for i in range(T_TILES + SCALE_LAG):
+        nc.vector.tensor_copy(out=mag_col[:], in_=mag_turned[:, 0:O_TILES])
+        nc.scalar.sqrt(norm[:], norm_sq[:])
+        lora_out(0, 1, lora(0, 1))
+        for i in range(1, EARLY):
+            quantise_tokens(i)
+        nc.vector.reciprocal(out=inv_norm[:], in_=norm[:])
+        nc.vector.tensor_tensor(out=m_col[:], in0=inv_norm[:], in1=mag_col[:], op=ALU.mult)
+        for i in range(T_TILES + 1):
             if i < T_TILES:
-                lora_products(i)
-                if i == 0:
-                    nc.scalar.sqrt(norm[:], norm_sq[:])
+                if i > 0:
+                    lora_out(i, 0, lora(i, 0))
+                    lora_out(i, 1, lora(i, 1))
                 if i + EARLY < T_TILES:
-                    group_words(
-                        False,
-                        x_grouped_words[:, i + EARLY, :, :, :],
-                        turn_words(x_words[:, i + EARLY, :]),
-                    )
-                add_base_products(i)
+                    group_x(i + EARLY, turn_x(i + EARLY))
+                banks = [base(i, 0), base(i, 1)]
+                add_base(i, 0, banks[0])
+                add_base(i, 1, banks[1])
                 if i + EARLY < T_TILES:
                     quantise_tokens(i + EARLY)
             if i == 0:
-                inv_norm = keep.tile([P, O_TILES], F32)
-                nc.vector.reciprocal(out=inv_norm[:], in_=norm[:])
-                m_col = keep.tile([P, O_TILES], F32)
-                nc.vector.tensor_tensor(out=m_col[:], in0=inv_norm[:], in1=mag_col[:], op=ALU.mult)
-            if i == 1:
-                m_turned = psum.tile([P, O_TILES_PER_HALF, P], F32, tag="bank")
+                m_turned = psum.tile([P, O_TILES_PER_HALF, P], F32, tag="bank", name="m_turned")
                 for j in range(O_TILES):
-                    half, j_in_half = divmod(j, O_TILES_PER_HALF)
+                    half, jh = divmod(j, O_TILES_PER_HALF)
                     nc.tensor.transpose(
-                        (m_turned, m_second)[half][:, j_in_half, :],
-                        m_col[:, j : j + 1].to_broadcast([P, P]),
-                        ident_f32[:],
+                        (m_turned, m_second)[half][:, jh, :], m_col[:, j : j + 1].to_broadcast([P, P]), ident_f32[:]
                     )
-                nc.scalar.copy(out=m_first[:], in_=m_turned[:].rearrange("p j o -> p (j o)"))
-            if i >= SCALE_LAG:
-                scale_and_store(i - SCALE_LAG)
+                nc.scalar.copy(out=m_sb[:, 0:BANK], in_=m_turned[:].rearrange("p j o -> p (j o)"))
+                nc.scalar.copy(
+                    out=m_sb[:, BANK:G_COLS],
+                    in_=m_second[:].rearrange("p j o -> p (j o)")[:, 0 : G_COLS - BANK],
+                )
+            if i >= 1:
+                scale_and_store(i - 1)

@@ -28,8 +28,8 @@ HALVES = D_OUT // BANK
 O_TILES_PER_HALF = BANK // P
 WORD_BLOCKS = D_IN // 2 // P
 
-STRIDED_W = 2
-STRIDED_X = 0
+STRIDED_W = 8
+STRIDED_X = 8
 MERGED = (4, 5, 6, 7)
 SCALAR_W = (0, 1)
 VECTOR_X = (0,)

@@ -28,15 +28,12 @@ HALVES = D_OUT // BANK
 O_TILES_PER_HALF = BANK // P
 WORD_BLOCKS = D_IN // 2 // P
 
-STRIDED_W = 8
-STRIDED_X = 8
-MERGED = (4, 5, 6, 7)
-SCALAR_W = (0, 1)
-VECTOR_X = (0,)
+MERGED = (3, 5, 7)
+SCALAR_W = (0, 1, 6)
+VECTOR_X = (1, 4)
 G_COLS = 640
 EARLY = 4
-LATE = 0
-W_BEFORE_X = 8
+LATE = 1
 
 FLOPS = 2 * TOKENS * D_IN * D_OUT + 2 * TOKENS * RANK * D_OUT + 2 * D_OUT * RANK * D_IN
 
@@ -81,25 +78,26 @@ def tile_loralinear_pa_kernel(tc, x, weight, a_w, b_w, magnitude, h_lora, out):
         nc.sync.dma_start(out=a_sb[:], in_=a_w)
         load_w(1)
         nc.sync.dma_start(out=b_sb[:, 4:8, :], in_=b_rows[:, 4:8, :])
-        for j in range(2, W_BEFORE_X):
-            load_w(j)
-        nc.sync.dma_start(out=h_sb[:], in_=h_rows)
+        load_w(2)
+        load_w(3)
+        load_w(4)
         load_x(0, 1)
+        load_w(5)
+        nc.sync.dma_start(out=h_sb[:], in_=h_rows)
+        load_w(6)
+        load_w(7)
         load_x(1, 1)
-        for j in range(W_BEFORE_X, O_TILES):
-            load_w(j)
+        load_x(2, 2)
         nc.sync.dma_start(
             out=mag_rows[0:O_TILES, :], in_=magnitude.rearrange("one (j p) -> (one j) p", p=P)
         )
-        for i in (2, 4, 6):
-            load_x(i, 2)
-        w_words = w_sb[:].bitcast(U32)
-        x_words = x_sb[:].bitcast(U32)
+        load_x(4, 2)
+        load_x(6, 2)
+        w_words = w_sb[:].bitcast(F32)
+        x_words = x_sb[:].bitcast(F32)
 
         b2T = keep.tile([P, D_OUT], BF16)
         hT = keep.tile([P, T_TILES, P], BF16)
-        w_ordered = keep.tile([P, O_TILES, D_IN // 2], U32)
-        x_ordered = keep.tile([P, T_TILES, D_IN // 2], U32)
         w_grouped = keep.tile([P, HALVES, PASSES, BANK, PACK], BF16, align_bytes=64)
         w_grouped_words = w_grouped[:].bitcast(F32)
         w_codes = keep.tile([P, HALVES, PASSES, BANK], U32, align_bytes=64)
@@ -114,24 +112,8 @@ def tile_loralinear_pa_kernel(tc, x, weight, a_w, b_w, magnitude, h_lora, out):
         m_second = psum_kept.tile([P, O_TILES_PER_HALF, P], F32)
         results = keep.tile([P, T_TILES, D_OUT], F32)
 
-        def order_words(ordered, words):
-            nc.gpsimd.tensor_copy(
-                out=ordered.rearrange("p (g u q) -> p g u q", g=PASSES, u=2),
-                in_=words.rearrange("p (g q u) -> p g u q", g=PASSES, u=2),
-            )
-
-        def turn_ordered(ordered):
+        def turn_words(words):
             bank = psum.tile([P, WORD_BLOCKS, P], F32, tag="bank")
-            ordered = ordered.bitcast(F32)
-            for blk in range(WORD_BLOCKS):
-                nc.tensor.transpose(
-                    bank[:, blk, :], ordered[:, blk * P : (blk + 1) * P], ident_f32[:]
-                )
-            return bank
-
-        def turn_strided(words):
-            bank = psum.tile([P, WORD_BLOCKS, P], F32, tag="bank")
-            words = words.bitcast(F32)
             for blk in range(WORD_BLOCKS):
                 g, u = divmod(blk, 2)
                 nc.tensor.transpose(
@@ -146,18 +128,16 @@ def tile_loralinear_pa_kernel(tc, x, weight, a_w, b_w, magnitude, h_lora, out):
             else:
                 nc.scalar.copy(out=grouped_words, in_=side_by_side)
 
-        def turn_w(j):
-            return turn_strided(w_words[:, j, :]) if j < STRIDED_W else turn_ordered(w_ordered[:, j, :])
-
-        def turn_x(i):
-            return turn_strided(x_words[:, i, :]) if i < STRIDED_X else turn_ordered(x_ordered[:, i, :])
-
-        def group_w(j, bank):
+        def turn_weight(j):
             half, jh = divmod(j, O_TILES_PER_HALF)
-            group_words(j not in SCALAR_W, w_grouped_words[:, half, :, jh * P : (jh + 1) * P, :], bank)
+            group_words(
+                j not in SCALAR_W,
+                w_grouped_words[:, half, :, jh * P : (jh + 1) * P, :],
+                turn_words(w_words[:, j, :]),
+            )
 
-        def group_x(i, bank):
-            group_words(i in VECTOR_X, x_grouped_words[:, i, :, :, :], bank)
+        def turn_tokens(i):
+            group_words(i in VECTOR_X, x_grouped_words[:, i, :, :, :], turn_words(x_words[:, i, :]))
 
         def quantise_weight(half):
             nc.vector.quantize_mx(
@@ -213,12 +193,10 @@ def tile_loralinear_pa_kernel(tc, x, weight, a_w, b_w, magnitude, h_lora, out):
             cols = slice(half * BANK, (half + 1) * BANK)
             bank = psum.tile([P, BANK], F32, tag="bank")
             nc.tensor.matmul(out=bank[:], lhsT=hT[:, i, :], rhs=b2T[:, cols], start=True, stop=True)
-            return bank
+            nc.scalar.copy(out=results[:, i, cols], in_=bank[:])
 
-        def lora_out(i, half, bank):
-            nc.scalar.copy(out=results[:, i, half * BANK : (half + 1) * BANK], in_=bank[:])
-
-        def base(i, half):
+        def add_base(i, half):
+            cols = slice(half * BANK, (half + 1) * BANK)
             bank = psum.tile([P, BANK], F32, tag="bank")
             for g in range(PASSES):
                 nc.tensor.matmul_mx(
@@ -230,10 +208,6 @@ def tile_loralinear_pa_kernel(tc, x, weight, a_w, b_w, magnitude, h_lora, out):
                     start=(g == 0),
                     stop=(g == PASSES - 1),
                 )
-            return bank
-
-        def add_base(i, half, bank):
-            cols = slice(half * BANK, (half + 1) * BANK)
             nc.vector.tensor_tensor(
                 out=results[:, i, cols], in0=bank[:], in1=results[:, i, cols], op=ALU.add
             )
@@ -270,83 +244,88 @@ def tile_loralinear_pa_kernel(tc, x, weight, a_w, b_w, magnitude, h_lora, out):
         m_col = keep.tile([P, O_TILES], F32)
         mag_col = keep.tile([P, O_TILES], F32)
 
-        for j in range(STRIDED_W, O_TILES):
-            order_words(w_ordered[:, j, :], w_words[:, j, :])
-        for i in range(STRIDED_X, T_TILES):
-            order_words(x_ordered[:, i, :], x_words[:, i, :])
+        def spread_m():
+            m_turned = psum.tile([P, O_TILES_PER_HALF, P], F32, tag="bank", name="m_turned")
+            for j in range(O_TILES):
+                half, jh = divmod(j, O_TILES_PER_HALF)
+                nc.tensor.transpose(
+                    (m_turned, m_second)[half][:, jh, :],
+                    m_col[:, j : j + 1].to_broadcast([P, P]),
+                    ident_f32[:],
+                )
+            nc.scalar.copy(out=m_sb[:, 0:BANK], in_=m_turned[:].rearrange("p j o -> p (j o)"))
+            nc.scalar.copy(
+                out=m_sb[:, BANK:G_COLS],
+                in_=m_second[:].rearrange("p j o -> p (j o)")[:, 0 : G_COLS - BANK],
+            )
 
-        late = []
+        waiting = []
 
-        def flush(n=0):
-            while len(late) > n:
-                sum_squares(*late.pop(0))
+        def square_waiting(keep_back):
+            while len(waiting) > keep_back:
+                sum_squares(*waiting.pop(0))
 
-        def weight_step(j):
-            w_turned = turn_w(j)
-            if j == 1:
-                turn_b(1)
+        def weight_norms(j):
             banks = products(j)
             w_eff = merged.tile([P, D_IN], F32)
-            group_w(j, w_turned)
             if j not in MERGED:
                 merge_weight(j, banks, w_eff)
-                late.append((j, banks, w_eff))
-                flush(LATE)
+                waiting.append((j, banks, w_eff))
+                square_waiting(LATE)
             else:
-                flush(LATE)
+                square_waiting(LATE)
                 sum_squares(j, banks, w_eff)
 
         turn_b(0)
         for j in range(O_TILES):
-            weight_step(j)
-            if j == 4:
-                quantise_weight(0)
+            if j == 2:
+                turn_b(1)
             if j == 5:
+                quantise_weight(0)
+                turn_tokens(0)
+            if j == 7:
                 h_turned = psum.tile([P, T_TILES, P], BF16, tag="bank")
                 for i in range(T_TILES):
                     nc.tensor.transpose(h_turned[:, i, :], h_sb[:, i, :], ident_bf16[:])
                 nc.vector.tensor_copy(out=hT[:], in_=h_turned[:])
-        for i in range(EARLY):
-            group_x(i, turn_x(i))
-        flush(0)
+                square_waiting(0)
+            turn_weight(j)
+            weight_norms(j)
+        turn_tokens(1)
         mag_turned = psum.tile([P, P], BF16, tag="bank")
         nc.tensor.transpose(mag_turned[:], mag_rows[:], ident_bf16[:])
-        lora_out(0, 0, lora(0, 0))
-        quantise_tokens(0)
+        nc.vector.tensor_copy(out=mag_col[:], in_=mag_turned[:, 0:O_TILES])
+        turn_tokens(2)
         quantise_weight(1)
+        quantise_tokens(0)
+        turn_tokens(3)
         nc.vector.tensor_tensor(
             out=norm_sq[:], in0=norm_sq_parts[:, 0, :], in1=norm_sq_parts[:, 1, :], op=ALU.add
         )
-        nc.vector.tensor_copy(out=mag_col[:], in_=mag_turned[:, 0:O_TILES])
         nc.scalar.sqrt(norm[:], norm_sq[:])
-        lora_out(0, 1, lora(0, 1))
-        for i in range(1, EARLY):
-            quantise_tokens(i)
-        nc.vector.reciprocal(out=inv_norm[:], in_=norm[:])
-        nc.vector.tensor_tensor(out=m_col[:], in0=inv_norm[:], in1=mag_col[:], op=ALU.mult)
+        quantise_tokens(1)
         for i in range(T_TILES + 1):
             if i < T_TILES:
-                if i > 0:
-                    lora_out(i, 0, lora(i, 0))
-                    lora_out(i, 1, lora(i, 1))
+                if i != 1:
+                    lora(i, 0)
+                    lora(i, 1)
+                if i == 0:
+                    quantise_tokens(2)
+                    quantise_tokens(3)
+                    nc.vector.reciprocal(out=inv_norm[:], in_=norm[:])
+                    nc.vector.tensor_tensor(
+                        out=m_col[:], in0=inv_norm[:], in1=mag_col[:], op=ALU.mult
+                    )
                 if i + EARLY < T_TILES:
-                    group_x(i + EARLY, turn_x(i + EARLY))
-                banks = [base(i, 0), base(i, 1)]
-                add_base(i, 0, banks[0])
-                add_base(i, 1, banks[1])
+                    turn_tokens(i + EARLY)
+                if i == 0:
+                    lora(1, 0)
+                add_base(i, 0)
+                add_base(i, 1)
+                if i == 0:
+                    lora(1, 1)
+                    spread_m()
                 if i + EARLY < T_TILES:
                     quantise_tokens(i + EARLY)
-            if i == 0:
-                m_turned = psum.tile([P, O_TILES_PER_HALF, P], F32, tag="bank", name="m_turned")
-                for j in range(O_TILES):
-                    half, jh = divmod(j, O_TILES_PER_HALF)
-                    nc.tensor.transpose(
-                        (m_turned, m_second)[half][:, jh, :], m_col[:, j : j + 1].to_broadcast([P, P]), ident_f32[:]
-                    )
-                nc.scalar.copy(out=m_sb[:, 0:BANK], in_=m_turned[:].rearrange("p j o -> p (j o)"))
-                nc.scalar.copy(
-                    out=m_sb[:, BANK:G_COLS],
-                    in_=m_second[:].rearrange("p j o -> p (j o)")[:, 0 : G_COLS - BANK],
-                )
             if i >= 1:
                 scale_and_store(i - 1)

@@ -33,6 +33,13 @@ SCALAR_W = (0, 1, 6)
 VECTOR_X = (1, 4)
 G_COLS = 640
 EARLY = 4
+B_HI = 2
+G_LAST = 512
+G_SIX = 512
+SPREAD_AT = 0
+MCOL_AT = 0
+TAIL = 1
+WHOLE = 5
 LATE = 1
 
 FLOPS = 2 * TOKENS * D_IN * D_OUT + 2 * TOKENS * RANK * D_OUT + 2 * D_OUT * RANK * D_IN
@@ -213,28 +220,31 @@ def tile_loralinear_pa_kernel(tc, x, weight, a_w, b_w, magnitude, h_lora, out):
             )
 
         def scale_and_store(i):
-            split = G_COLS if i < T_TILES - 1 else BANK
+            split = G_LAST if i == T_TILES - 1 else (G_SIX if i == T_TILES - 2 else G_COLS)
             nc.gpsimd.tensor_tensor(
                 out=results[:, i, 0:split], in0=results[:, i, 0:split], in1=m_sb[:, 0:split], op=ALU.mult
             )
-            nc.sync.dma_start(out=out_rows[:, i, 0:split], in_=results[:, i, 0:split])
+            if i >= WHOLE:
+                nc.sync.dma_start(out=out_rows[:, i, 0:split], in_=results[:, i, 0:split])
             nc.vector.tensor_tensor(
                 out=results[:, i, split:D_OUT],
                 in0=m_second[:].rearrange("p j o -> p (j o)")[:, split - BANK : BANK],
                 in1=results[:, i, split:D_OUT],
                 op=ALU.mult,
             )
-            nc.sync.dma_start(out=out_rows[:, i, split:D_OUT], in_=results[:, i, split:D_OUT])
+            if i >= WHOLE:
+                nc.sync.dma_start(out=out_rows[:, i, split:D_OUT], in_=results[:, i, split:D_OUT])
+            else:
+                nc.sync.dma_start(out=out_rows[:, i, :], in_=results[:, i, :])
 
-        def turn_b(half):
+        def turn_b(first, last):
+            count = last - first
             b_turned = psum.tile([P, O_TILES_PER_HALF, P], BF16, tag="bank")
-            for jh in range(O_TILES_PER_HALF):
-                nc.tensor.transpose(
-                    b_turned[:, jh, :], b_sb[:, half * O_TILES_PER_HALF + jh, :], ident_bf16[:]
-                )
+            for n in range(count):
+                nc.tensor.transpose(b_turned[:, n, :], b_sb[:, first + n, :], ident_bf16[:])
             nc.vector.tensor_scalar(
-                out=b2T[:, half * BANK : (half + 1) * BANK],
-                in0=b_turned[:].rearrange("r j o -> r (j o)"),
+                out=b2T[:, first * P : last * P],
+                in0=b_turned[:, 0:count, :].rearrange("r j o -> r (j o)"),
                 scalar1=SCALING, scalar2=None, op0=ALU.mult,
             )
 
@@ -276,10 +286,10 @@ def tile_loralinear_pa_kernel(tc, x, weight, a_w, b_w, magnitude, h_lora, out):
                 square_waiting(LATE)
                 sum_squares(j, banks, w_eff)
 
-        turn_b(0)
+        turn_b(0, 4)
         for j in range(O_TILES):
-            if j == 2:
-                turn_b(1)
+            if j == B_HI:
+                turn_b(4, 8)
             if j == 5:
                 quantise_weight(0)
                 turn_tokens(0)
@@ -312,6 +322,7 @@ def tile_loralinear_pa_kernel(tc, x, weight, a_w, b_w, magnitude, h_lora, out):
                 if i == 0:
                     quantise_tokens(2)
                     quantise_tokens(3)
+                if i == MCOL_AT:
                     nc.vector.reciprocal(out=inv_norm[:], in_=norm[:])
                     nc.vector.tensor_tensor(
                         out=m_col[:], in0=inv_norm[:], in1=mag_col[:], op=ALU.mult
@@ -321,11 +332,14 @@ def tile_loralinear_pa_kernel(tc, x, weight, a_w, b_w, magnitude, h_lora, out):
                 if i == 0:
                     lora(1, 0)
                 add_base(i, 0)
+                if i == T_TILES - 1 and TAIL:
+                    scale_and_store(i - 1)
                 add_base(i, 1)
                 if i == 0:
                     lora(1, 1)
+                if i == SPREAD_AT:
                     spread_m()
                 if i + EARLY < T_TILES:
                     quantise_tokens(i + EARLY)
-            if i >= 1:
+            if i > SPREAD_AT and not (i == T_TILES - 1 and TAIL):
                 scale_and_store(i - 1)

from contextlib import ExitStack

import concourse.mybir as mybir
from concourse.masks import make_identity

F32 = mybir.dt.float32
BF16 = mybir.dt.bfloat16
U32 = mybir.dt.uint32
U8 = mybir.dt.uint8
FP8X4 = mybir.dt.float8_e4m3fn_x4
ACT = mybir.ActivationFunctionType
ALU = mybir.AluOpType

P = 128
PACK = 4
BANK = 512

TOKENS = 1024
D_IN = 1024
D_OUT = 1024
RANK = 128
SCALING = 2.0

T_TILES = TOKENS // P
O_TILES = D_OUT // P
PASSES = D_IN // (P * PACK)
HALVES = D_OUT // BANK
O_TILES_PER_HALF = BANK // P
WORD_BLOCKS = D_IN // 2 // P

MERGED = (3, 5, 7)
SCALAR_W = (0, 1, 6)
VECTOR_X = (1, 4)
G_COLS = 640
EARLY = 4
B_HI = 2
G_LAST = 512
G_SIX = 512
SPREAD_AT = 0
MCOL_AT = 0
TAIL = 1
WHOLE = 5
LATE = 1

FLOPS = 2 * TOKENS * D_IN * D_OUT + 2 * TOKENS * RANK * D_OUT + 2 * D_OUT * RANK * D_IN

def tile_loralinear_pa_kernel(tc, x, weight, a_w, b_w, magnitude, h_lora, out):
    nc = tc.nc
    x_rows = x.flatten_outer_dims().rearrange("(p i) d -> p i d", i=T_TILES)
    h_rows = h_lora.flatten_outer_dims().rearrange("(p i) r -> p i r", i=T_TILES)
    out_rows = out.flatten_outer_dims().rearrange("(p i) o -> p i o", i=T_TILES)
    b_rows = b_w.rearrange("(j p) r -> p j r", p=P)

    with ExitStack() as ctx:
        keep = ctx.enter_context(tc.tile_pool(name="keep", bufs=1))
        merged = ctx.enter_context(tc.tile_pool(name="merged", bufs=4))
        psum = ctx.enter_context(tc.psum_pool(name="psum", bufs=7))
        psum_kept = ctx.enter_context(tc.psum_pool(name="psum_kept", bufs=1))
        ctx.enter_context(tc.manual_schedule())

        ident_bf16 = keep.tile([P, P], BF16)
        make_identity(nc, ident_bf16[:])
        ident_f32 = keep.tile([P, P], F32)
        make_identity(nc, ident_f32[:])
        table_warmer = keep.tile([P, 1], F32)
        nc.vector.memset(table_warmer[:], 1.0)
        nc.scalar.sqrt(table_warmer[:], table_warmer[:])
        mag_rows = keep.tile([P, P], BF16)
        nc.vector.memset(mag_rows[:], 0.0)

        b_sb = keep.tile([P, O_TILES, RANK], BF16)
        a_sb = keep.tile([P, D_IN], BF16)
        w_sb = keep.tile([P, O_TILES, D_IN], BF16)
        h_sb = keep.tile([P, T_TILES, RANK], BF16)
        x_sb = keep.tile([P, T_TILES, D_IN], BF16)

        def load_w(j):
            nc.sync.dma_start(out=w_sb[:, j, :], in_=weight[j * P : (j + 1) * P, :])

        def load_x(i, n):
            nc.sync.dma_start(out=x_sb[:, i : i + n, :], in_=x_rows[:, i : i + n, :])

        nc.sync.dma_start(out=b_sb[:, 0:4, :], in_=b_rows[:, 0:4, :])
        load_w(0)
        nc.sync.dma_start(out=a_sb[:], in_=a_w)
        load_w(1)
        nc.sync.dma_start(out=b_sb[:, 4:8, :], in_=b_rows[:, 4:8, :])
        load_w(2)
        load_w(3)
        load_w(4)
        load_x(0, 1)
        load_w(5)
        nc.sync.dma_start(out=h_sb[:], in_=h_rows)
        load_w(6)
        load_w(7)
        load_x(1, 1)
        load_x(2, 2)
        nc.sync.dma_start(
            out=mag_rows[0:O_TILES, :], in_=magnitude.rearrange("one (j p) -> (one j) p", p=P)
        )
        load_x(4, 2)
        load_x(6, 2)
        w_words = w_sb[:].bitcast(F32)
        x_words = x_sb[:].bitcast(F32)

        b2T = keep.tile([P, D_OUT], BF16)
        hT = keep.tile([P, T_TILES, P], BF16)
        w_grouped = keep.tile([P, HALVES, PASSES, BANK, PACK], BF16, align_bytes=64)
        w_grouped_words = w_grouped[:].bitcast(F32)
        w_codes = keep.tile([P, HALVES, PASSES, BANK], U32, align_bytes=64)
        w_scales = keep.tile([P, HALVES, PASSES, BANK], U8, align_bytes=64)
        x_grouped = keep.tile([P, T_TILES, PASSES, P, PACK], BF16, align_bytes=64)
        x_grouped_words = x_grouped[:].bitcast(F32)
        x_codes = keep.tile([P, T_TILES, PASSES, P], U32, align_bytes=64)
        x_scales = keep.tile([P, T_TILES, PASSES, P], U8, align_bytes=64)
        norm_sq_parts = keep.tile([P, D_IN // BANK, O_TILES], F32)
        nc.vector.memset(norm_sq_parts[:], 0.0)
        m_sb = keep.tile([P, G_COLS], F32)
        m_second = psum_kept.tile([P, O_TILES_PER_HALF, P], F32)
        results = keep.tile([P, T_TILES, D_OUT], F32)

        def turn_words(words):
            bank = psum.tile([P, WORD_BLOCKS, P], F32, tag="bank")
            for blk in range(WORD_BLOCKS):
                g, u = divmod(blk, 2)
                nc.tensor.transpose(
                    bank[:, blk, :], words[:, 2 * P * g + u : 2 * P * (g + 1) : 2], ident_f32[:]
                )
            return bank

        def group_words(on_vector, grouped_words, bank):
            side_by_side = bank[:].rearrange("p (g u) r -> p g r u", u=2)
            if on_vector:
                nc.vector.tensor_copy(out=grouped_words, in_=side_by_side)
            else:
                nc.scalar.copy(out=grouped_words, in_=side_by_side)

        def turn_weight(j):
            half, jh = divmod(j, O_TILES_PER_HALF)
            group_words(
                j not in SCALAR_W,
                w_grouped_words[:, half, :, jh * P : (jh + 1) * P, :],
                turn_words(w_words[:, j, :]),
            )

        def turn_tokens(i):
            group_words(i in VECTOR_X, x_grouped_words[:, i, :, :, :], turn_words(x_words[:, i, :]))

        def quantise_weight(half):
            nc.vector.quantize_mx(
                out=w_codes[:, half, :, :].rearrange("p g o -> p (g o)").bitcast(FP8X4),
                scales=w_scales[:, half, :, :].rearrange("p g o -> p (g o)"),
                in_=w_grouped[:, half, :, :, :].rearrange("p g o t -> p (g o t)"),
            )

        def quantise_tokens(i):
            nc.vector.quantize_mx(
                out=x_codes[:, i, :, :].rearrange("p g r -> p (g r)").bitcast(FP8X4),
                scales=x_scales[:, i, :, :].rearrange("p g r -> p (g r)"),
                in_=x_grouped[:, i, :, :, :].rearrange("p g r t -> p (g r t)"),
            )

        def products(j):
            banks = []
            for c in range(D_IN // BANK):
                cols = slice(c * BANK, (c + 1) * BANK)
                ba2 = psum.tile([P, BANK], F32, tag="bank", name="ba2")
                if j in MERGED:
                    nc.tensor.matmul(
                        out=ba2[:], lhsT=ident_bf16[:], rhs=w_sb[:, j, cols], start=True, stop=False
                    )
                nc.tensor.matmul(
                    out=ba2[:], lhsT=b2T[:, j * P : (j + 1) * P], rhs=a_sb[:, cols],
                    start=(j not in MERGED), stop=True,
                )
                banks.append(ba2)
            return banks

        def merge_weight(j, banks, w_eff):
            for c in range(D_IN // BANK):
                cols = slice(c * BANK, (c + 1) * BANK)
                nc.vector.tensor_tensor(
                    out=w_eff[:, cols], in0=banks[c][:], in1=w_sb[:, j, cols], op=ALU.add
                )

        def sum_squares(j, banks, w_eff):
            if j in MERGED:
                for c in range(D_IN // BANK):
                    nc.scalar.activation(
                        out=w_eff[:, c * BANK : (c + 1) * BANK], in_=banks[c][:], func=ACT.Square,
                        accum_out=norm_sq_parts[:, c, j : j + 1],
                    )
            else:
                nc.scalar.activation(
                    out=w_eff[:], in_=w_eff[:], func=ACT.Square,
                    accum_out=norm_sq_parts[:, 0, j : j + 1],
                )

        def lora(i, half):
            cols = slice(half * BANK, (half + 1) * BANK)
            bank = psum.tile([P, BANK], F32, tag="bank")
            nc.tensor.matmul(out=bank[:], lhsT=hT[:, i, :], rhs=b2T[:, cols], start=True, stop=True)
            nc.scalar.copy(out=results[:, i, cols], in_=bank[:])

        def add_base(i, half):
            cols = slice(half * BANK, (half + 1) * BANK)
            bank = psum.tile([P, BANK], F32, tag="bank")
            for g in range(PASSES):
                nc.tensor.matmul_mx(
                    out=bank[:],
                    lhsT=x_codes[:, i, g, :].bitcast(FP8X4),
                    lhsT_scale=x_scales[:, i, g, :],
                    rhs=w_codes[:, half, g, :].bitcast(FP8X4),
                    rhs_scale=w_scales[:, half, g, :],
                    start=(g == 0),
                    stop=(g == PASSES - 1),
                )
            nc.vector.tensor_tensor(
                out=results[:, i, cols], in0=bank[:], in1=results[:, i, cols], op=ALU.add
            )

        def scale_and_store(i):
            split = G_LAST if i == T_TILES - 1 else (G_SIX if i == T_TILES - 2 else G_COLS)
            nc.gpsimd.tensor_tensor(
                out=results[:, i, 0:split], in0=results[:, i, 0:split], in1=m_sb[:, 0:split], op=ALU.mult
            )
            if i >= WHOLE:
                nc.sync.dma_start(out=out_rows[:, i, 0:split], in_=results[:, i, 0:split])
            nc.vector.tensor_tensor(
                out=results[:, i, split:D_OUT],
                in0=m_second[:].rearrange("p j o -> p (j o)")[:, split - BANK : BANK],
                in1=results[:, i, split:D_OUT],
                op=ALU.mult,
            )
            if i >= WHOLE:
                nc.sync.dma_start(out=out_rows[:, i, split:D_OUT], in_=results[:, i, split:D_OUT])
            else:
                nc.sync.dma_start(out=out_rows[:, i, :], in_=results[:, i, :])

        def turn_b(first, last):
            count = last - first
            b_turned = psum.tile([P, O_TILES_PER_HALF, P], BF16, tag="bank")
            for n in range(count):
                nc.tensor.transpose(b_turned[:, n, :], b_sb[:, first + n, :], ident_bf16[:])
            nc.vector.tensor_scalar(
                out=b2T[:, first * P : last * P],
                in0=b_turned[:, 0:count, :].rearrange("r j o -> r (j o)"),
                scalar1=SCALING, scalar2=None, op0=ALU.mult,
            )

        norm_sq = keep.tile([P, O_TILES], F32)
        norm = keep.tile([P, O_TILES], F32)
        inv_norm = keep.tile([P, O_TILES], F32)
        m_col = keep.tile([P, O_TILES], F32)
        mag_col = keep.tile([P, O_TILES], F32)

        def spread_m():
            m_turned = psum.tile([P, O_TILES_PER_HALF, P], F32, tag="bank", name="m_turned")
            for j in range(O_TILES):
                half, jh = divmod(j, O_TILES_PER_HALF)
                nc.tensor.transpose(
                    (m_turned, m_second)[half][:, jh, :],
                    m_col[:, j : j + 1].to_broadcast([P, P]),
                    ident_f32[:],
                )
            nc.scalar.copy(out=m_sb[:, 0:BANK], in_=m_turned[:].rearrange("p j o -> p (j o)"))
            nc.scalar.copy(
                out=m_sb[:, BANK:G_COLS],
                in_=m_second[:].rearrange("p j o -> p (j o)")[:, 0 : G_COLS - BANK],
            )

        waiting = []

        def square_waiting(keep_back):
            while len(waiting) > keep_back:
                sum_squares(*waiting.pop(0))

        def weight_norms(j):
            banks = products(j)
            w_eff = merged.tile([P, D_IN], F32)
            if j not in MERGED:
                merge_weight(j, banks, w_eff)
                waiting.append((j, banks, w_eff))
                square_waiting(LATE)
            else:
                square_waiting(LATE)
                sum_squares(j, banks, w_eff)

        turn_b(0, 4)
        for j in range(O_TILES):
            if j == B_HI:
                turn_b(4, 8)
            if j == 5:
                quantise_weight(0)
                turn_tokens(0)
            if j == 7:
                h_turned = psum.tile([P, T_TILES, P], BF16, tag="bank")
                for i in range(T_TILES):
                    nc.tensor.transpose(h_turned[:, i, :], h_sb[:, i, :], ident_bf16[:])
                nc.vector.tensor_copy(out=hT[:], in_=h_turned[:])
                square_waiting(0)
            turn_weight(j)
            weight_norms(j)
        turn_tokens(1)
        mag_turned = psum.tile([P, P], BF16, tag="bank")
        nc.tensor.transpose(mag_turned[:], mag_rows[:], ident_bf16[:])
        nc.vector.tensor_copy(out=mag_col[:], in_=mag_turned[:, 0:O_TILES])
        turn_tokens(2)
        quantise_weight(1)
        quantise_tokens(0)
        turn_tokens(3)
        nc.vector.tensor_tensor(
            out=norm_sq[:], in0=norm_sq_parts[:, 0, :], in1=norm_sq_parts[:, 1, :], op=ALU.add
        )
        nc.scalar.sqrt(norm[:], norm_sq[:])
        quantise_tokens(1)
        for i in range(T_TILES + 1):
            if i < T_TILES:
                if i != 1:
                    lora(i, 0)
                    lora(i, 1)
                if i == 0:
                    quantise_tokens(2)
                    quantise_tokens(3)
                if i == MCOL_AT:
                    nc.vector.reciprocal(out=inv_norm[:], in_=norm[:])
                    nc.vector.tensor_tensor(
                        out=m_col[:], in0=inv_norm[:], in1=mag_col[:], op=ALU.mult
                    )
                if i + EARLY < T_TILES:
                    turn_tokens(i + EARLY)
                if i == 0:
                    lora(1, 0)
                add_base(i, 0)
                if i == T_TILES - 1 and TAIL:
                    scale_and_store(i - 1)
                add_base(i, 1)
                if i == 0:
                    lora(1, 1)
                if i == SPREAD_AT:
                    spread_m()
                if i + EARLY < T_TILES:
                    quantise_tokens(i + EARLY)
            if i > SPREAD_AT and not (i == T_TILES - 1 and TAIL):
                scale_and_store(i - 1)
